import numpy as np
import ml_dtypes


def mxq(x, axis, fmt="e4m3"):
    dtype, down = {"e4m3": (ml_dtypes.float8_e4m3fn, 7), "e5m2": (ml_dtypes.float8_e5m2, 14)}[fmt]
    v = np.moveaxis(np.asarray(x, np.float32).astype(ml_dtypes.bfloat16).astype(np.float64), axis, -1)
    blocks = v.reshape(v.shape[:-1] + (-1, 32))
    amax = np.abs(blocks).max(-1, keepdims=True)
    byte = np.maximum(np.where(amax > 0, np.frexp(amax)[1] - 1 + 127, 0) - down, 1)
    scale = np.exp2(byte - 127.0)
    codes = (blocks / scale).astype(np.float32).astype(dtype).astype(np.float64)
    return np.moveaxis((codes * scale).reshape(v.shape), -1, axis)


WIDE = False


def mx_kscale(k):
    if not WIDE:
        return np.ones(k)
    levels = np.array([10, -10, 5, -5, 0])
    if k % 512:
        return np.exp2(np.random.permutation(np.resize(levels, k // 32))).repeat(32)
    a = np.empty((k // 512, 16))
    for p in range(k // 512):
        a[p, :8] = np.random.permutation(np.resize(levels, 8))
        for g in range(8):
            far = levels[np.abs(levels - a[p, g]) >= 10]
            a[p, g + 8] = far[np.random.randint(len(far))]
    return np.exp2(a.ravel()).repeat(32)


BF16 = ml_dtypes.bfloat16


def bf(x):
    return np.asarray(x, np.float32).astype(BF16)


def f64(x):
    return np.asarray(x).astype(np.float64)


B, D_IN, H, D_OUT, DEPTH, Q = 8192, 1024, 512, 1024, 3, 2


def quantum_probs(qw):
    n = qw.shape[1]
    s0r, s0i, s1r, s1i = np.ones(n), np.zeros(n), np.zeros(n), np.zeros(n)
    for d in range(qw.shape[0]):
        th = qw[d, :, 0, 0]
        ph = qw[d, :, 1, 1]
        c, s = np.cos(th), np.sin(th)
        n0r, n0i = c * s0r - s * s1r, c * s0i - s * s1i
        n1r, n1i = s * s0r + c * s1r, s * s0i + c * s1i
        cp, sp = np.cos(ph), np.sin(ph)
        s0r, s0i = n0r, n0i
        s1r, s1i = n1r * cp - n1i * sp, n1r * sp + n1i * cp
    return s0r * s0r + s0i * s0i


def setup_inputs():
    s, t = mx_kscale(H), mx_kscale(H)
    return {"h0": bf(np.maximum(np.random.standard_normal((B, H)), 0.0) * s),
            "w1": bf(np.random.standard_normal((H, H)) * 1.4 / np.sqrt(H) / s[:, None] * t),
            "b1": bf(np.random.standard_normal(H) * 0.3 * t),
            "q1_qw": bf(np.random.standard_normal((DEPTH, H, Q, Q))),
            "q1_cw": bf(np.random.standard_normal((H, H)) * 1.4 / np.sqrt(H) / t[:, None]),
            "q1_cb": bf(np.random.standard_normal(H) * 0.3)}


def reference(h0, w1, b1, q1_qw, q1_cw, q1_cb):
    h1 = np.maximum((mxq(f64(h0), 1, "e4m3") @ mxq(f64(w1), 0, "e4m3")) + f64(b1), 0.0)
    return np.tanh((mxq(h1, 1, "e4m3") @ mxq(f64(q1_cw), 0, "e4m3")) + f64(q1_cb) + quantum_probs(f64(q1_qw))[None, :])

@@ -1,0 +1,271 @@
+import math
+from contextlib import ExitStack
+
+import concourse.mybir as mybir
+from concourse.masks import make_identity
+
+F32 = mybir.dt.float32
+BF16 = mybir.dt.bfloat16
+U32 = mybir.dt.uint32
+U8 = mybir.dt.uint8
+FP8X4 = mybir.dt.float8_e4m3fn_x4
+ACT = mybir.ActivationFunctionType
+ALU = mybir.AluOpType
+
+P = 128
+PACK = 4
+BATCH = 8192
+H = P * PACK
+DEPTH = 3
+ROWS = 512
+SUB = ROWS // P
+ROUNDS = BATCH // ROWS
+ROUND_TO_INT = 1.5 * 2.0**23
+COS = 0
+SIN = 1
+THETA = 0
+PHI = 1
+COPY_LAG = 1
+FIRST_LAG = 2
+REGROUP_LAG = 3
+SECOND_LAG = 4
+
+FLOPS = 2 * 2 * BATCH * H * H
+
+
+def quantise(nc, pool, grouped, name):
+    columns = grouped.shape[1] // PACK
+    words = pool.tile([P, columns], U32, name=name + "_words", align_bytes=64)
+    scales = pool.tile([P, columns], U8, name=name + "_scales", align_bytes=64)
+    nc.vector.quantize_mx(out=words[:].bitcast(FP8X4), scales=scales[:], in_=grouped)
+    return words, scales
+
+
+def output_bias_column(nc, small, q1_qw, q1_cb):
+    angles = small.tile([P, DEPTH, PACK * 4], BF16, name="angles")
+    nc.scalar.dma_start(out=angles[:], in_=q1_qw.rearrange("d (q i) a b -> q d (i a b)", i=PACK))
+    cb = small.tile([P, PACK], BF16, name="cb")
+    nc.scalar.dma_start(out=cb[:], in_=q1_cb.rearrange("(q i) -> q i", i=PACK))
+
+    diagonal = angles[:].rearrange("q d (i e) -> q (d i) e", e=4)[:, :, 0:4:3]
+    turns = small.tile([P, 2, DEPTH * PACK, 2], F32, name="turns")
+    nc.vector.tensor_scalar(
+        out=turns[:, COS], in0=diagonal, scalar1=0.5 / math.pi, scalar2=0.25, op0=ALU.mult, op1=ALU.add
+    )
+    nc.vector.tensor_scalar(
+        out=turns[:, SIN], in0=diagonal, scalar1=0.5 / math.pi, scalar2=0.0, op0=ALU.mult, op1=ALU.add
+    )
+    whole = small.tile([P, 2, DEPTH * PACK, 2], F32, name="whole")
+    nc.vector.tensor_scalar(
+        out=whole[:], in0=turns[:], scalar1=ROUND_TO_INT, scalar2=ROUND_TO_INT, op0=ALU.add, op1=ALU.subtract
+    )
+    part = small.tile([P, 2, DEPTH * PACK, 2], F32, name="part")
+    nc.vector.tensor_tensor(out=part[:], in0=turns[:], in1=whole[:], op=ALU.subtract)
+    trig = small.tile([P, 2, DEPTH * PACK, 2], F32, name="trig")
+    nc.scalar.activation(out=trig[:], in_=part[:], func=ACT.Sin, scale=2.0 * math.pi)
+
+    def layer(d):
+        return slice(d * PACK, (d + 1) * PACK)
+
+    def rotation(kind, d):
+        return trig[:, kind, layer(d), THETA].unsqueeze(1).to_broadcast([P, 2, PACK])
+
+    a0 = small.tile([P, 2, PACK], F32, name="a0_first")
+    nc.gpsimd.memset(a0[:, 1, :], 0.0)
+    nc.gpsimd.tensor_copy(out=a0[:, 0, :], in_=trig[:, COS, layer(0), THETA])
+    a1 = small.tile([P, 2, PACK], F32, name="a1_first")
+    nc.gpsimd.tensor_tensor(out=a1[:], in0=trig[:, :, layer(0), PHI], in1=rotation(SIN, 0), op=ALU.mult)
+    for d in range(1, DEPTH):
+        cos_a0 = small.tile([P, 2, PACK], F32)
+        sin_a1 = small.tile([P, 2, PACK], F32)
+        new_a0 = small.tile([P, 2, PACK], F32)
+        nc.gpsimd.tensor_tensor(out=cos_a0[:], in0=a0[:], in1=rotation(COS, d), op=ALU.mult)
+        nc.gpsimd.tensor_tensor(out=sin_a1[:], in0=a1[:], in1=rotation(SIN, d), op=ALU.mult)
+        nc.gpsimd.tensor_tensor(out=new_a0[:], in0=cos_a0[:], in1=sin_a1[:], op=ALU.subtract)
+        if d < DEPTH - 1:
+            sin_a0 = small.tile([P, 2, PACK], F32)
+            cos_a1 = small.tile([P, 2, PACK], F32)
+            turned = small.tile([P, 2, PACK], F32)
+            nc.gpsimd.tensor_tensor(out=sin_a0[:], in0=a0[:], in1=rotation(SIN, d), op=ALU.mult)
+            nc.gpsimd.tensor_tensor(out=cos_a1[:], in0=a1[:], in1=rotation(COS, d), op=ALU.mult)
+            nc.gpsimd.tensor_tensor(out=turned[:], in0=sin_a0[:], in1=cos_a1[:], op=ALU.add)
+            by_cos = small.tile([P, 2, PACK], F32)
+            by_sin = small.tile([P, 2, PACK], F32)
+            new_a1 = small.tile([P, 2, PACK], F32)
+            cos_phi = trig[:, COS, layer(d), PHI].unsqueeze(1).to_broadcast([P, 2, PACK])
+            sin_phi = trig[:, SIN, layer(d), PHI].unsqueeze(1).to_broadcast([P, 2, PACK])
+            nc.gpsimd.tensor_tensor(out=by_cos[:], in0=turned[:], in1=cos_phi, op=ALU.mult)
+            nc.gpsimd.tensor_tensor(out=by_sin[:], in0=turned[:], in1=sin_phi, op=ALU.mult)
+            nc.gpsimd.tensor_tensor(out=new_a1[:, 0, :], in0=by_cos[:, 0, :], in1=by_sin[:, 1, :], op=ALU.subtract)
+            nc.gpsimd.tensor_tensor(out=new_a1[:, 1, :], in0=by_sin[:, 0, :], in1=by_cos[:, 1, :], op=ALU.add)
+            a1 = new_a1
+        a0 = new_a0
+    squares = small.tile([P, 2, PACK], F32, name="squares")
+    nc.gpsimd.tensor_tensor(out=squares[:], in0=a0[:], in1=a0[:], op=ALU.mult)
+    prob = small.tile([P, PACK], F32, name="prob")
+    nc.gpsimd.tensor_tensor(out=prob[:], in0=squares[:, 0, :], in1=squares[:, 1, :], op=ALU.add)
+    bias_column = small.tile([P, PACK], F32, name="bias_column")
+    nc.gpsimd.tensor_tensor(out=bias_column[:], in0=prob[:], in1=cb[:], op=ALU.add)
+    return bias_column
+
+
+def tile_quantumneuralnetwork_pa_t_kernel(tc, h0, w1, b1, q1_qw, q1_cw, q1_cb, out):
+    nc = tc.nc
+    with ExitStack() as ctx:
+        ctx.enter_context(tc.manual_schedule())
+        keep = ctx.enter_context(tc.tile_pool(name="keep", bufs=1))
+        small = ctx.enter_context(tc.tile_pool(name="small", bufs=2))
+        rows_in = ctx.enter_context(tc.tile_pool(name="rows_in", bufs=ROUNDS))
+        work = ctx.enter_context(tc.tile_pool(name="work", bufs=3))
+        single = ctx.enter_context(tc.tile_pool(name="single", bufs=1))
+        rows_out = ctx.enter_context(tc.tile_pool(name="rows_out", bufs=4))
+        psum_t = ctx.enter_context(tc.psum_pool(name="psum_t", bufs=2))
+        psum_1 = ctx.enter_context(tc.psum_pool(name="psum_1", bufs=3))
+        psum_2 = ctx.enter_context(tc.psum_pool(name="psum_2", bufs=3))
+
+        h0_rounds = h0.rearrange("(g c r) k -> g c (r k)", c=P, r=SUB)
+        out_rounds = out.rearrange("(g c r) n -> g c r n", c=P, r=SUB)
+
+        w1_raw = keep.tile([P, PACK, H], BF16, name="w1_raw")
+        nc.sync.dma_start(out=w1_raw[:], in_=w1.rearrange("(q t) j -> q t j", t=PACK))
+        x_tiles = []
+        for g in range(ROUNDS):
+            x_tiles.append(rows_in.tile([P, SUB * H], BF16, name="x"))
+        nc.sync.dma_start(out=x_tiles[0][:], in_=h0_rounds[0])
+        nc.sync.dma_start(out=x_tiles[1][:], in_=h0_rounds[1])
+        cw_raw = keep.tile([P, PACK, H], BF16, name="cw_raw")
+        nc.sync.dma_start(out=cw_raw[:], in_=q1_cw.rearrange("(q t) n -> q t n", t=PACK))
+        for g in range(2, ROUNDS):
+            nc.sync.dma_start(out=x_tiles[g][:], in_=h0_rounds[g])
+
+        ident = keep.tile([P, P], F32, name="ident")
+        make_identity(nc, ident[:])
+        b1_raw = small.tile([P, PACK], BF16, name="b1_raw")
+        nc.scalar.dma_start(out=b1_raw[:], in_=b1.rearrange("(q t) -> q t", t=PACK))
+        bias_column = output_bias_column(nc, small, q1_qw, q1_cb)
+        b1_column = keep.tile([P, PACK], F32, name="b1_column")
+        nc.vector.tensor_copy(out=b1_column[:], in_=b1_raw[:])
+
+        w1_grouped = keep.tile([P, H, PACK], BF16, name="w1_grouped", align_bytes=64)
+        nc.vector.tensor_copy(
+            out=w1_grouped[:].rearrange("q (t m) k -> q t m k", t=PACK),
+            in_=w1_raw[:].rearrange("q k (m t) -> q t m k", t=PACK),
+        )
+        w1_words, w1_scales = quantise(nc, keep, w1_grouped[:].rearrange("q j k -> q (j k)"), "w1")
+
+        flipped, h0_grouped, h0_packed, h1_planes, h1_grouped, h1_packed, results = {}, {}, {}, {}, {}, {}, {}
+
+        def transpose_rows(g):
+            x_words = x_tiles[g][:].bitcast(F32)
+            for half in range(2):
+                flipped[g, half] = psum_t.tile([P, 2, 2, P], F32, name="flipped")
+                for r in range(2):
+                    for u in range(2):
+                        row = (2 * half + r) * 2 * P
+                        nc.tensor.transpose(
+                            out=flipped[g, half][:, r, u, :],
+                            in_=x_words[:, row + u : row + 2 * P : 2],
+                            identity=ident[:],
+                        )
+
+        def empty_bank(g, half):
+            if half == 0:
+                h0_grouped[g] = work.tile([P, ROWS * PACK], BF16, name="h0_grouped", align_bytes=64)
+            h0_pairs = h0_grouped[g][:].bitcast(F32).rearrange("q (h r c u) -> q h r c u", h=2, r=2, u=2)
+            nc.vector.tensor_copy(out=h0_pairs[:, half], in_=flipped[g, half][:].rearrange("q r u c -> q r c u"))
+
+        def quantise_h0(g):
+            h0_packed[g] = quantise(nc, work, h0_grouped[g][:], "h0")
+
+        def first_product(g, t):
+            h0_words, h0_scales = h0_packed[g]
+            if t == 0:
+                h1_planes[g] = work.tile([P, PACK, ROWS], BF16, name="h1_planes")
+            product1 = psum_1.tile([P, ROWS], F32, name="product1")
+            nc.tensor.matmul_mx(
+                out=product1[:],
+                lhsT=w1_words[:, t * P : (t + 1) * P].bitcast(FP8X4),
+                lhsT_scale=w1_scales[:, t * P : (t + 1) * P],
+                rhs=h0_words[:].bitcast(FP8X4),
+                rhs_scale=h0_scales[:],
+                start=True,
+                stop=True,
+            )
+            nc.scalar.activation(
+                out=h1_planes[g][:, t, :], in_=product1[:], func=ACT.Relu, bias=b1_column[:, t : t + 1], scale=1.0
+            )
+
+        def regroup_h1(g):
+            h1_grouped[g] = single.tile([P, ROWS, PACK], BF16, name="h1_grouped", align_bytes=64)
+            nc.gpsimd.tensor_scalar(
+                out=h1_grouped[g][:].rearrange("q (c i) t -> q c t i", i=4),
+                in0=h1_planes[g][:].rearrange("q t (c i) -> q c t i", i=4),
+                scalar1=1.0,
+                scalar2=0.0,
+                op0=ALU.mult,
+                op1=ALU.add,
+            )
+
+        def quantise_h1(g):
+            h1_packed[g] = quantise(nc, work, h1_grouped[g][:].rearrange("q c t -> q (c t)"), "h1")
+
+        def second_product(g, r):
+            h1_words, h1_scales = h1_packed[g]
+            if r == 0:
+                results[g] = rows_out.tile([P, SUB, H], F32, name="y")
+            product2 = psum_2.tile([P, H], F32, name="product2")
+            nc.tensor.matmul_mx(
+                out=product2[:],
+                lhsT=h1_words[:, r * P : (r + 1) * P].bitcast(FP8X4),
+                lhsT_scale=h1_scales[:, r * P : (r + 1) * P],
+                rhs=cw_words[:].bitcast(FP8X4),
+                rhs_scale=cw_scales[:],
+                start=True,
+                stop=True,
+            )
+            nc.vector.tensor_tensor(out=results[g][:, r, :], in0=product2[:], in1=bias_row[:], op=ALU.add)
+
+        def tanh_and_store(g, r):
+            nc.scalar.activation(out=results[g][:, r, :], in_=results[g][:, r, :], func=ACT.Tanh)
+            nc.sync.dma_start(out=out_rounds[g][:, r, :], in_=results[g][:, r, :])
+
+        def pipeline_step(step):
+            def at(lag, stage, *args):
+                if 0 <= step - lag < ROUNDS:
+                    stage(step - lag, *args)
+
+            at(SECOND_LAG, quantise_h1)
+            at(REGROUP_LAG, regroup_h1)
+            at(COPY_LAG, empty_bank, 0)
+            at(COPY_LAG, empty_bank, 1)
+            at(FIRST_LAG, first_product, 0)
+            for i in range(1, PACK):
+                at(FIRST_LAG, first_product, i)
+                at(SECOND_LAG, second_product, i - 1)
+            at(SECOND_LAG, second_product, SUB - 1)
+            for r in range(SUB):
+                at(SECOND_LAG, tanh_and_store, r)
+            at(0, transpose_rows)
+            at(COPY_LAG, quantise_h0)
+
+        for step in range(REGROUP_LAG):
+            pipeline_step(step)
+        cw_grouped = keep.tile([P, H, PACK], BF16, name="cw_grouped", align_bytes=64)
+        nc.vector.tensor_copy(out=cw_grouped[:], in_=cw_raw[:].rearrange("q t n -> q n t"))
+        cw_words, cw_scales = quantise(nc, keep, cw_grouped[:].rearrange("q n t -> q (n t)"), "cw")
+        pipeline_step(REGROUP_LAG)
+        spread = psum_2.tile([P, PACK, P], F32, name="spread", tag="product2")
+        for i in range(PACK):
+            nc.tensor.matmul(
+                out=spread[:, i, :],
+                lhsT=bias_column[:, i : i + 1].to_broadcast([P, P]),
+                rhs=ident[:],
+                start=True,
+                stop=True,
+            )
+        bias_row = keep.tile([P, H], F32, name="bias_row")
+        nc.vector.tensor_copy(
+            out=bias_row[:].rearrange("p (q i) -> p q i", i=PACK), in_=spread[:].rearrange("p i q -> p q i")
+        )
+        for step in range(SECOND_LAG, ROUNDS + SECOND_LAG):
+            pipeline_step(step)

@@ -41,12 +41,7 @@ def quantise(nc, pool, grouped, name):
     return words, scales
 
 
-def output_bias_column(nc, small, q1_qw, q1_cb):
-    angles = small.tile([P, DEPTH, PACK * 4], BF16, name="angles")
-    nc.scalar.dma_start(out=angles[:], in_=q1_qw.rearrange("d (q i) a b -> q d (i a b)", i=PACK))
-    cb = small.tile([P, PACK], BF16, name="cb")
-    nc.scalar.dma_start(out=cb[:], in_=q1_cb.rearrange("(q i) -> q i", i=PACK))
-
+def output_bias_column(nc, small, angles, cb):
     diagonal = angles[:].rearrange("q d (i e) -> q (d i) e", e=4)[:, :, 0:4:3]
     turns = small.tile([P, 2, DEPTH * PACK, 2], F32, name="turns")
     nc.vector.tensor_scalar(
@@ -63,6 +58,8 @@ def output_bias_column(nc, small, q1_qw, q1_cb):
     nc.vector.tensor_tensor(out=part[:], in0=turns[:], in1=whole[:], op=ALU.subtract)
     trig = small.tile([P, 2, DEPTH * PACK, 2], F32, name="trig")
     nc.scalar.activation(out=trig[:], in_=part[:], func=ACT.Sin, scale=2.0 * math.pi)
+    first_tanh = small.tile([P, 1], F32, name="first_tanh")
+    nc.scalar.activation(out=first_tanh[:], in_=part[:, COS, 0, THETA : THETA + 1], func=ACT.Tanh)
 
     def layer(d):
         return slice(d * PACK, (d + 1) * PACK)
@@ -126,12 +123,22 @@ def tile_quantumneuralnetwork_pa_t_kernel(tc, h0, w1, b1, q1_qw, q1_cw, q1_cb, o
         h0_rounds = h0.rearrange("(g c r) k -> g c (r k)", c=P, r=SUB)
         out_rounds = out.rearrange("(g c r) n -> g c r n", c=P, r=SUB)
 
-        w1_raw = keep.tile([P, PACK, H], BF16, name="w1_raw")
-        nc.sync.dma_start(out=w1_raw[:], in_=w1.rearrange("(q t) j -> q t j", t=PACK))
+        angles = small.tile([P, DEPTH, PACK * 4], BF16, name="angles")
+        nc.scalar.dma_start(out=angles[:], in_=q1_qw.rearrange("d (q i) a b -> q d (i a b)", i=PACK))
+        b1_column = keep.tile([P, PACK], BF16, name="b1_column")
+        nc.scalar.dma_start(out=b1_column[:], in_=b1.rearrange("(q t) -> q t", t=PACK))
+        cb = small.tile([P, PACK], BF16, name="cb")
+        nc.scalar.dma_start(out=cb[:], in_=q1_cb.rearrange("(q i) -> q i", i=PACK))
+
         x_tiles = []
         for g in range(ROUNDS):
             x_tiles.append(rows_in.tile([P, SUB * H], BF16, name="x"))
-        nc.sync.dma_start(out=x_tiles[0][:], in_=h0_rounds[0])
+        half_row = SUB * H // 2
+        for half in range(2):
+            piece = slice(half * half_row, (half + 1) * half_row)
+            nc.sync.dma_start(out=x_tiles[0][:, piece], in_=h0_rounds[0][:, piece])
+        w1_raw = keep.tile([P, PACK, H], BF16, name="w1_raw")
+        nc.sync.dma_start(out=w1_raw[:], in_=w1.rearrange("(q t) j -> q t j", t=PACK))
         nc.sync.dma_start(out=x_tiles[1][:], in_=h0_rounds[1])
         cw_raw = keep.tile([P, PACK, H], BF16, name="cw_raw")
         nc.sync.dma_start(out=cw_raw[:], in_=q1_cw.rearrange("(q t) n -> q t n", t=PACK))
@@ -140,24 +147,31 @@ def tile_quantumneuralnetwork_pa_t_kernel(tc, h0, w1, b1, q1_qw, q1_cw, q1_cb, o
 
         ident = keep.tile([P, P], F32, name="ident")
         make_identity(nc, ident[:])
-        b1_raw = small.tile([P, PACK], BF16, name="b1_raw")
-        nc.scalar.dma_start(out=b1_raw[:], in_=b1.rearrange("(q t) -> q t", t=PACK))
-        bias_column = output_bias_column(nc, small, q1_qw, q1_cb)
-        b1_column = keep.tile([P, PACK], F32, name="b1_column")
-        nc.vector.tensor_copy(out=b1_column[:], in_=b1_raw[:])
 
         w1_grouped = keep.tile([P, H, PACK], BF16, name="w1_grouped", align_bytes=64)
-        nc.vector.tensor_copy(
-            out=w1_grouped[:].rearrange("q (t m) k -> q t m k", t=PACK),
-            in_=w1_raw[:].rearrange("q k (m t) -> q t m k", t=PACK),
-        )
-        w1_words, w1_scales = quantise(nc, keep, w1_grouped[:].rearrange("q j k -> q (j k)"), "w1")
+        w1_words = keep.tile([P, H], U32, name="w1_words", align_bytes=64)
+        w1_scales = keep.tile([P, H], U8, name="w1_scales", align_bytes=64)
+
+        def group_w1(half):
+            columns = slice(half * H // 2, (half + 1) * H // 2)
+            nc.vector.tensor_copy(
+                out=w1_grouped[:, columns].rearrange("q (t m) k -> q t m k", m=P),
+                in_=w1_raw[:].rearrange("q k (m t) -> q t m k", t=PACK)[:, 2 * half : 2 * half + 2],
+            )
+
+        def quantise_w1(half):
+            columns = slice(half * H // 2, (half + 1) * H // 2)
+            nc.vector.quantize_mx(
+                out=w1_words[:, columns].bitcast(FP8X4),
+                scales=w1_scales[:, columns],
+                in_=w1_grouped[:, columns].rearrange("q j k -> q (j k)"),
+            )
 
         flipped, h0_grouped, h0_packed, h1_planes, h1_grouped, h1_packed, results = {}, {}, {}, {}, {}, {}, {}
 
-        def transpose_rows(g):
+        def transpose_rows(g, halves=(0, 1)):
             x_words = x_tiles[g][:].bitcast(F32)
-            for half in range(2):
+            for half in halves:
                 flipped[g, half] = psum_t.tile([P, 2, 2, P], F32, name="flipped")
                 for r in range(2):
                     for u in range(2):
@@ -168,11 +182,11 @@ def tile_quantumneuralnetwork_pa_t_kernel(tc, h0, w1, b1, q1_qw, q1_cw, q1_cb, o
                             identity=ident[:],
                         )
 
-        def empty_bank(g, half):
+        def empty_bank(g, half, copy=nc.vector.tensor_copy):
             if half == 0:
                 h0_grouped[g] = work.tile([P, ROWS * PACK], BF16, name="h0_grouped", align_bytes=64)
             h0_pairs = h0_grouped[g][:].bitcast(F32).rearrange("q (h r c u) -> q h r c u", h=2, r=2, u=2)
-            nc.vector.tensor_copy(out=h0_pairs[:, half], in_=flipped[g, half][:].rearrange("q r u c -> q r c u"))
+            copy(out=h0_pairs[:, half], in_=flipped[g, half][:].rearrange("q r u c -> q r c u"))
 
         def quantise_h0(g):
             h0_packed[g] = quantise(nc, work, h0_grouped[g][:], "h0")
@@ -195,9 +209,9 @@ def tile_quantumneuralnetwork_pa_t_kernel(tc, h0, w1, b1, q1_qw, q1_cw, q1_cb, o
                 out=h1_planes[g][:, t, :], in_=product1[:], func=ACT.Relu, bias=b1_column[:, t : t + 1], scale=1.0
             )
 
-        def regroup_h1(g):
+        def regroup_h1(g, engine=nc.gpsimd):
             h1_grouped[g] = single.tile([P, ROWS, PACK], BF16, name="h1_grouped", align_bytes=64)
-            nc.gpsimd.tensor_scalar(
+            engine.tensor_scalar(
                 out=h1_grouped[g][:].rearrange("q (c i) t -> q c t i", i=4),
                 in0=h1_planes[g][:].rearrange("q t (c i) -> q c t i", i=4),
                 scalar1=1.0,
@@ -229,9 +243,11 @@ def tile_quantumneuralnetwork_pa_t_kernel(tc, h0, w1, b1, q1_qw, q1_cw, q1_cb, o
             nc.scalar.activation(out=results[g][:, r, :], in_=results[g][:, r, :], func=ACT.Tanh)
             nc.sync.dma_start(out=out_rounds[g][:, r, :], in_=results[g][:, r, :])
 
+        AHEAD = {transpose_rows: 4, empty_bank: 4, quantise_h0: 3, first_product: 3, regroup_h1: 2, quantise_h1: 1}
+
         def pipeline_step(step):
             def at(lag, stage, *args):
-                if 0 <= step - lag < ROUNDS:
+                if AHEAD.get(stage, 0) <= step - lag < ROUNDS:
                     stage(step - lag, *args)
 
             at(SECOND_LAG, quantise_h1)
@@ -248,24 +264,50 @@ def tile_quantumneuralnetwork_pa_t_kernel(tc, h0, w1, b1, q1_qw, q1_cw, q1_cb, o
             at(0, transpose_rows)
             at(COPY_LAG, quantise_h0)
 
-        for step in range(REGROUP_LAG):
-            pipeline_step(step)
         cw_grouped = keep.tile([P, H, PACK], BF16, name="cw_grouped", align_bytes=64)
+        transpose_rows(0)
+        output_bias = output_bias_column(nc, small, angles, cb)
+        empty_bank(0, 0)
+        empty_bank(0, 1, nc.scalar.copy)
+        group_w1(0)
+        quantise_h0(0)
+        quantise_w1(0)
+        group_w1(1)
+        transpose_rows(1)
+        empty_bank(1, 0)
+        quantise_w1(1)
+        for t in range(PACK):
+            first_product(0, t)
+        empty_bank(1, 1)
+        transpose_rows(2)
+        quantise_h0(1)
+        for t in range(PACK):
+            first_product(1, t)
+        empty_bank(2, 0)
+        empty_bank(2, 1)
         nc.vector.tensor_copy(out=cw_grouped[:], in_=cw_raw[:].rearrange("q t n -> q n t"))
-        cw_words, cw_scales = quantise(nc, keep, cw_grouped[:].rearrange("q n t -> q (n t)"), "cw")
-        pipeline_step(REGROUP_LAG)
+        quantise_h0(2)
         spread = psum_2.tile([P, PACK, P], F32, name="spread", tag="product2")
         for i in range(PACK):
             nc.tensor.matmul(
                 out=spread[:, i, :],
-                lhsT=bias_column[:, i : i + 1].to_broadcast([P, P]),
+                lhsT=output_bias[:, i : i + 1].to_broadcast([P, P]),
                 rhs=ident[:],
                 start=True,
                 stop=True,
             )
+        for t in range(PACK):
+            first_product(2, t)
+        transpose_rows(3)
+        regroup_h1(0, nc.vector)
+        cw_words, cw_scales = quantise(nc, keep, cw_grouped[:].rearrange("q n t -> q (n t)"), "cw")
+        quantise_h1(0)
         bias_row = keep.tile([P, H], F32, name="bias_row")
         nc.vector.tensor_copy(
             out=bias_row[:].rearrange("p (q i) -> p q i", i=PACK), in_=spread[:].rearrange("p i q -> p q i")
         )
+        regroup_h1(1)
+        empty_bank(3, 0, nc.scalar.copy)
+        empty_bank(3, 1, nc.scalar.copy)
         for step in range(SECOND_LAG, ROUNDS + SECOND_LAG):
             pipeline_step(step)

@@ -28,6 +28,7 @@ PHI = 1
 COPY_LAG = 1
 FIRST_LAG = 2
 REGROUP_LAG = 3
+TANH_LAG = 5
 SECOND_LAG = 4
 
 FLOPS = 2 * 2 * BATCH * H * H
@@ -254,13 +255,18 @@ def tile_quantumneuralnetwork_pa_t_kernel(tc, h0, w1, b1, q1_qw, q1_cw, q1_cb, o
             at(REGROUP_LAG, regroup_h1)
             at(COPY_LAG, empty_bank, 0)
             at(COPY_LAG, empty_bank, 1)
+            at(TANH_LAG, tanh_and_store, 2)
+            at(TANH_LAG, tanh_and_store, 3)
             at(FIRST_LAG, first_product, 0)
-            for i in range(1, PACK):
-                at(FIRST_LAG, first_product, i)
-                at(SECOND_LAG, second_product, i - 1)
-            at(SECOND_LAG, second_product, SUB - 1)
-            for r in range(SUB):
-                at(SECOND_LAG, tanh_and_store, r)
+            at(SECOND_LAG, second_product, 0)
+            at(FIRST_LAG, first_product, 1)
+            at(SECOND_LAG, second_product, 1)
+            at(FIRST_LAG, first_product, 2)
+            at(SECOND_LAG, second_product, 2)
+            at(SECOND_LAG, tanh_and_store, 0)
+            at(FIRST_LAG, first_product, 3)
+            at(SECOND_LAG, second_product, 3)
+            at(SECOND_LAG, tanh_and_store, 1)
             at(0, transpose_rows)
             at(COPY_LAG, quantise_h0)
 
@@ -309,5 +315,5 @@ def tile_quantumneuralnetwork_pa_t_kernel(tc, h0, w1, b1, q1_qw, q1_cw, q1_cb, o
         regroup_h1(1)
         empty_bank(3, 0, nc.scalar.copy)
         empty_bank(3, 1, nc.scalar.copy)
-        for step in range(SECOND_LAG, ROUNDS + SECOND_LAG):
+        for step in range(SECOND_LAG, ROUNDS + TANH_LAG):
             pipeline_step(step)

@@ -125,12 +125,7 @@ def tile_quantumneuralnetwork_pa_t_kernel(tc, h0, w1, b1, q1_qw, q1_cw, q1_cb, o
         out_rounds = out.rearrange("(g c r) n -> g c r n", c=P, r=SUB)
 
         angles = small.tile([P, DEPTH, PACK * 4], BF16, name="angles")
-        nc.scalar.dma_start(out=angles[:], in_=q1_qw.rearrange("d (q i) a b -> q d (i a b)", i=PACK))
-        b1_column = keep.tile([P, PACK], BF16, name="b1_column")
-        nc.scalar.dma_start(out=b1_column[:], in_=b1.rearrange("(q t) -> q t", t=PACK))
-        cb = small.tile([P, PACK], BF16, name="cb")
-        nc.scalar.dma_start(out=cb[:], in_=q1_cb.rearrange("(q i) -> q i", i=PACK))
-
+        nc.sync.dma_start(out=angles[:], in_=q1_qw.rearrange("d (q i) a b -> q d (i a b)", i=PACK))
         x_tiles = []
         for g in range(ROUNDS):
             x_tiles.append(rows_in.tile([P, SUB * H], BF16, name="x"))
@@ -140,6 +135,10 @@ def tile_quantumneuralnetwork_pa_t_kernel(tc, h0, w1, b1, q1_qw, q1_cw, q1_cb, o
             nc.sync.dma_start(out=x_tiles[0][:, piece], in_=h0_rounds[0][:, piece])
         w1_raw = keep.tile([P, PACK, H], BF16, name="w1_raw")
         nc.sync.dma_start(out=w1_raw[:], in_=w1.rearrange("(q t) j -> q t j", t=PACK))
+        b1_column = keep.tile([P, PACK], BF16, name="b1_column")
+        nc.sync.dma_start(out=b1_column[:], in_=b1.rearrange("(q t) -> q t", t=PACK))
+        cb = small.tile([P, PACK], BF16, name="cb")
+        nc.sync.dma_start(out=cb[:], in_=q1_cb.rearrange("(q i) -> q i", i=PACK))
         nc.sync.dma_start(out=x_tiles[1][:], in_=h0_rounds[1])
         cw_raw = keep.tile([P, PACK, H], BF16, name="cw_raw")
         nc.sync.dma_start(out=cw_raw[:], in_=q1_cw.rearrange("(q t) n -> q t n", t=PACK))
@@ -153,9 +152,9 @@ def tile_quantumneuralnetwork_pa_t_kernel(tc, h0, w1, b1, q1_qw, q1_cw, q1_cb, o
         w1_words = keep.tile([P, H], U32, name="w1_words", align_bytes=64)
         w1_scales = keep.tile([P, H], U8, name="w1_scales", align_bytes=64)
 
-        def group_w1(half):
+        def group_w1(half, copy=nc.vector.tensor_copy):
             columns = slice(half * H // 2, (half + 1) * H // 2)
-            nc.vector.tensor_copy(
+            copy(
                 out=w1_grouped[:, columns].rearrange("q (t m) k -> q t m k", m=P),
                 in_=w1_raw[:].rearrange("q k (m t) -> q t m k", t=PACK)[:, 2 * half : 2 * half + 2],
             )
@@ -196,7 +195,10 @@ def tile_quantumneuralnetwork_pa_t_kernel(tc, h0, w1, b1, q1_qw, q1_cw, q1_cb, o
             h0_words, h0_scales = h0_packed[g]
             if t == 0:
                 h1_planes[g] = work.tile([P, PACK, ROWS], BF16, name="h1_planes")
-            product1 = psum_1.tile([P, ROWS], F32, name="product1")
+            if g < 2 and t == PACK - 1:
+                product1 = psum_2.tile([P, ROWS], F32, name="product1", tag="product2")
+            else:
+                product1 = psum_1.tile([P, ROWS], F32, name="product1")
             nc.tensor.matmul_mx(
                 out=product1[:],
                 lhsT=w1_words[:, t * P : (t + 1) * P].bitcast(FP8X4),
@@ -210,8 +212,8 @@ def tile_quantumneuralnetwork_pa_t_kernel(tc, h0, w1, b1, q1_qw, q1_cw, q1_cb, o
                 out=h1_planes[g][:, t, :], in_=product1[:], func=ACT.Relu, bias=b1_column[:, t : t + 1], scale=1.0
             )
 
-        def regroup_h1(g, engine=nc.gpsimd):
-            h1_grouped[g] = single.tile([P, ROWS, PACK], BF16, name="h1_grouped", align_bytes=64)
+        def regroup_h1(g, engine=nc.gpsimd, pool=single):
+            h1_grouped[g] = pool.tile([P, ROWS, PACK], BF16, name="h1_grouped", align_bytes=64)
             engine.tensor_scalar(
                 out=h1_grouped[g][:].rearrange("q (c i) t -> q c t i", i=4),
                 in0=h1_planes[g][:].rearrange("q t (c i) -> q c t i", i=4),
@@ -271,6 +273,13 @@ def tile_quantumneuralnetwork_pa_t_kernel(tc, h0, w1, b1, q1_qw, q1_cw, q1_cb, o
             at(COPY_LAG, quantise_h0)
 
         cw_grouped = keep.tile([P, H, PACK], BF16, name="cw_grouped", align_bytes=64)
+
+        def group_cw(half):
+            columns = slice(half * H // 2, (half + 1) * H // 2)
+            nc.vector.tensor_copy(
+                out=cw_grouped[:, columns], in_=cw_raw[:, :, columns].rearrange("q t n -> q n t")
+            )
+
         transpose_rows(0)
         output_bias = output_bias_column(nc, small, angles, cb)
         empty_bank(0, 0)
@@ -278,7 +287,7 @@ def tile_quantumneuralnetwork_pa_t_kernel(tc, h0, w1, b1, q1_qw, q1_cw, q1_cb, o
         group_w1(0)
         quantise_h0(0)
         quantise_w1(0)
-        group_w1(1)
+        group_w1(1, nc.scalar.copy)
         transpose_rows(1)
         empty_bank(1, 0)
         quantise_w1(1)
@@ -287,12 +296,13 @@ def tile_quantumneuralnetwork_pa_t_kernel(tc, h0, w1, b1, q1_qw, q1_cw, q1_cb, o
         empty_bank(1, 1)
         transpose_rows(2)
         quantise_h0(1)
+        group_cw(0)
         for t in range(PACK):
             first_product(1, t)
         empty_bank(2, 0)
         empty_bank(2, 1)
-        nc.vector.tensor_copy(out=cw_grouped[:], in_=cw_raw[:].rearrange("q t n -> q n t"))
         quantise_h0(2)
+        group_cw(1)
         spread = psum_2.tile([P, PACK, P], F32, name="spread", tag="product2")
         for i in range(PACK):
             nc.tensor.matmul(
@@ -302,9 +312,10 @@ def tile_quantumneuralnetwork_pa_t_kernel(tc, h0, w1, b1, q1_qw, q1_cw, q1_cb, o
                 start=True,
                 stop=True,
             )
-        for t in range(PACK):
+        for t in range(PACK - 1):
             first_product(2, t)
         transpose_rows(3)
+        first_product(2, PACK - 1)
         regroup_h1(0, nc.vector)
         cw_words, cw_scales = quantise(nc, keep, cw_grouped[:].rearrange("q n t -> q (n t)"), "cw")
         quantise_h1(0)
@@ -315,5 +326,26 @@ def tile_quantumneuralnetwork_pa_t_kernel(tc, h0, w1, b1, q1_qw, q1_cw, q1_cb, o
         regroup_h1(1)
         empty_bank(3, 0, nc.scalar.copy)
         empty_bank(3, 1, nc.scalar.copy)
-        for step in range(SECOND_LAG, ROUNDS + TANH_LAG):
+        for step in range(SECOND_LAG, ROUNDS + COPY_LAG):
             pipeline_step(step)
+
+        last = ROUNDS - 1
+        tanh_and_store(last - 3, 2)
+        quantise_h1(last - 2)
+        regroup_h1(last - 1)
+        for i in range(PACK):
+            first_product(last, i)
+            second_product(last - 2, i)
+        tanh_and_store(last - 3, 3)
+        for r in range(SUB):
+            tanh_and_store(last - 2, r)
+        quantise_h1(last - 1)
+        regroup_h1(last, nc.vector, work)
+        for r in range(SUB):
+            second_product(last - 1, r)
+            tanh_and_store(last - 1, r)
+            if r == 0:
+                quantise_h1(last)
+        for r in range(SUB):
+            second_product(last, r)
+            tanh_and_store(last, r)

@@ -145,6 +145,8 @@ def tile_quantumneuralnetwork_pa_t_kernel(tc, h0, w1, b1, q1_qw, q1_cw, q1_cb, o
         for g in range(2, ROUNDS):
             nc.sync.dma_start(out=x_tiles[g][:], in_=h0_rounds[g])
 
+        blank = keep.tile([P, ROWS], BF16, name="blank")
+        nc.vector.memset(blank[:], 0.0)
         ident = keep.tile([P, P], F32, name="ident")
         make_identity(nc, ident[:])
 
@@ -212,6 +214,10 @@ def tile_quantumneuralnetwork_pa_t_kernel(tc, h0, w1, b1, q1_qw, q1_cw, q1_cb, o
                 out=h1_planes[g][:, t, :], in_=product1[:], func=ACT.Relu, bias=b1_column[:, t : t + 1], scale=1.0
             )
 
+        def keep_clock(g):
+            unread = psum_1.tile([P, ROWS], F32, name="unread", tag="product1")
+            nc.tensor.matmul(out=unread[:], lhsT=blank[:, :P], rhs=blank[:], start=True, stop=True)
+
         def regroup_h1(g, engine=nc.gpsimd, pool=single):
             h1_grouped[g] = pool.tile([P, ROWS, PACK], BF16, name="h1_grouped", align_bytes=64)
             engine.tensor_scalar(
@@ -266,10 +272,11 @@ def tile_quantumneuralnetwork_pa_t_kernel(tc, h0, w1, b1, q1_qw, q1_cw, q1_cb, o
             at(FIRST_LAG, first_product, 2)
             at(SECOND_LAG, second_product, 2)
             at(SECOND_LAG, tanh_and_store, 0)
-            at(FIRST_LAG, first_product, 3)
             at(SECOND_LAG, second_product, 3)
             at(SECOND_LAG, tanh_and_store, 1)
+            at(FIRST_LAG, first_product, 3)
             at(0, transpose_rows)
+            at(FIRST_LAG, keep_clock)
             at(COPY_LAG, quantise_h0)
 
         cw_grouped = keep.tile([P, H, PACK], BF16, name="cw_grouped", align_bytes=64)

@@ -29,6 +29,7 @@ COPY_LAG = 1
 FIRST_LAG = 2
 REGROUP_LAG = 3
 TANH_LAG = 5
+ROWS_AHEAD = 2
 SECOND_LAG = 4
 
 FLOPS = 2 * 2 * BATCH * H * H
@@ -113,7 +114,7 @@ def tile_quantumneuralnetwork_pa_t_kernel(tc, h0, w1, b1, q1_qw, q1_cw, q1_cb, o
         ctx.enter_context(tc.manual_schedule())
         keep = ctx.enter_context(tc.tile_pool(name="keep", bufs=1))
         small = ctx.enter_context(tc.tile_pool(name="small", bufs=2))
-        rows_in = ctx.enter_context(tc.tile_pool(name="rows_in", bufs=ROUNDS))
+        rows_in = ctx.enter_context(tc.tile_pool(name="rows_in", bufs=ROWS_AHEAD + 1))
         work = ctx.enter_context(tc.tile_pool(name="work", bufs=3))
         single = ctx.enter_context(tc.tile_pool(name="single", bufs=1))
         rows_out = ctx.enter_context(tc.tile_pool(name="rows_out", bufs=4))
@@ -126,24 +127,27 @@ def tile_quantumneuralnetwork_pa_t_kernel(tc, h0, w1, b1, q1_qw, q1_cw, q1_cb, o
 
         angles = small.tile([P, DEPTH, PACK * 4], BF16, name="angles")
         nc.sync.dma_start(out=angles[:], in_=q1_qw.rearrange("d (q i) a b -> q d (i a b)", i=PACK))
-        x_tiles = []
-        for g in range(ROUNDS):
-            x_tiles.append(rows_in.tile([P, SUB * H], BF16, name="x"))
-        half_row = SUB * H // 2
-        for half in range(2):
-            piece = slice(half * half_row, (half + 1) * half_row)
-            nc.sync.dma_start(out=x_tiles[0][:, piece], in_=h0_rounds[0][:, piece])
+        x_tiles = {}
+
+        def load_rows(g, pieces=1):
+            x_tiles[g] = rows_in.tile([P, SUB * H], BF16, name="x")
+            width = SUB * H // pieces
+            for start in range(0, SUB * H, width):
+                nc.sync.dma_start(
+                    out=x_tiles[g][:, start : start + width], in_=h0_rounds[g][:, start : start + width]
+                )
+
+        load_rows(0, 2)
         w1_raw = keep.tile([P, PACK, H], BF16, name="w1_raw")
         nc.sync.dma_start(out=w1_raw[:], in_=w1.rearrange("(q t) j -> q t j", t=PACK))
         b1_column = keep.tile([P, PACK], BF16, name="b1_column")
         nc.sync.dma_start(out=b1_column[:], in_=b1.rearrange("(q t) -> q t", t=PACK))
         cb = small.tile([P, PACK], BF16, name="cb")
         nc.sync.dma_start(out=cb[:], in_=q1_cb.rearrange("(q i) -> q i", i=PACK))
-        nc.sync.dma_start(out=x_tiles[1][:], in_=h0_rounds[1])
+        load_rows(1)
         cw_raw = keep.tile([P, PACK, H], BF16, name="cw_raw")
         nc.sync.dma_start(out=cw_raw[:], in_=q1_cw.rearrange("(q t) n -> q t n", t=PACK))
-        for g in range(2, ROUNDS):
-            nc.sync.dma_start(out=x_tiles[g][:], in_=h0_rounds[g])
+        load_rows(2)
 
         blank = keep.tile([P, ROWS], BF16, name="blank")
         nc.vector.memset(blank[:], 0.0)
@@ -254,11 +258,14 @@ def tile_quantumneuralnetwork_pa_t_kernel(tc, h0, w1, b1, q1_qw, q1_cw, q1_cb, o
 
         AHEAD = {transpose_rows: 4, empty_bank: 4, quantise_h0: 3, first_product: 3, regroup_h1: 2, quantise_h1: 1}
 
+        AHEAD[load_rows] = 6
+
         def pipeline_step(step):
             def at(lag, stage, *args):
                 if AHEAD.get(stage, 0) <= step - lag < ROUNDS:
                     stage(step - lag, *args)
 
+            at(-ROWS_AHEAD, load_rows)
             at(SECOND_LAG, quantise_h1)
             at(REGROUP_LAG, regroup_h1)
             at(COPY_LAG, empty_bank, 0)
@@ -288,6 +295,7 @@ def tile_quantumneuralnetwork_pa_t_kernel(tc, h0, w1, b1, q1_qw, q1_cw, q1_cb, o
             )
 
         transpose_rows(0)
+        load_rows(3)
         output_bias = output_bias_column(nc, small, angles, cb)
         empty_bank(0, 0)
         empty_bank(0, 1, nc.scalar.copy)
@@ -296,12 +304,14 @@ def tile_quantumneuralnetwork_pa_t_kernel(tc, h0, w1, b1, q1_qw, q1_cw, q1_cb, o
         quantise_w1(0)
         group_w1(1, nc.scalar.copy)
         transpose_rows(1)
+        load_rows(4)
         empty_bank(1, 0)
         quantise_w1(1)
         for t in range(PACK):
             first_product(0, t)
         empty_bank(1, 1)
         transpose_rows(2)
+        load_rows(5)
         quantise_h0(1)
         group_cw(0)
         for t in range(PACK):

@@ -153,6 +153,8 @@ def tile_quantumneuralnetwork_pa_t_kernel(tc, h0, w1, b1, q1_qw, q1_cw, q1_cb, o
         nc.vector.memset(blank[:], 0.0)
         ident = keep.tile([P, P], F32, name="ident")
         make_identity(nc, ident[:])
+        first_sin = small.tile([P, 1], F32, name="first_sin")
+        nc.scalar.activation(out=first_sin[:], in_=blank[:, :1], func=ACT.Sin)
 
         w1_grouped = keep.tile([P, H, PACK], BF16, name="w1_grouped", align_bytes=64)
         w1_words = keep.tile([P, H], U32, name="w1_words", align_bytes=64)
@@ -252,9 +254,10 @@ def tile_quantumneuralnetwork_pa_t_kernel(tc, h0, w1, b1, q1_qw, q1_cw, q1_cb, o
             )
             nc.vector.tensor_tensor(out=results[g][:, r, :], in0=product2[:], in1=bias_row[:], op=ALU.add)
 
-        def tanh_and_store(g, r):
-            nc.scalar.activation(out=results[g][:, r, :], in_=results[g][:, r, :], func=ACT.Tanh)
-            nc.sync.dma_start(out=out_rounds[g][:, r, :], in_=results[g][:, r, :])
+        def tanh_and_store(g, r, count=1):
+            part = results[g][:, r : r + count, :]
+            nc.scalar.activation(out=part, in_=part, func=ACT.Tanh)
+            nc.sync.dma_start(out=out_rounds[g][:, r : r + count, :], in_=part)
 
         AHEAD = {transpose_rows: 4, empty_bank: 4, quantise_h0: 3, first_product: 3, regroup_h1: 2, quantise_h1: 1}
 
@@ -270,17 +273,15 @@ def tile_quantumneuralnetwork_pa_t_kernel(tc, h0, w1, b1, q1_qw, q1_cw, q1_cb, o
             at(REGROUP_LAG, regroup_h1)
             at(COPY_LAG, empty_bank, 0)
             at(COPY_LAG, empty_bank, 1)
-            at(TANH_LAG, tanh_and_store, 2)
-            at(TANH_LAG, tanh_and_store, 3)
+            at(TANH_LAG, tanh_and_store, 2, 2)
             at(FIRST_LAG, first_product, 0)
             at(SECOND_LAG, second_product, 0)
             at(FIRST_LAG, first_product, 1)
             at(SECOND_LAG, second_product, 1)
             at(FIRST_LAG, first_product, 2)
             at(SECOND_LAG, second_product, 2)
-            at(SECOND_LAG, tanh_and_store, 0)
+            at(SECOND_LAG, tanh_and_store, 0, 2)
             at(SECOND_LAG, second_product, 3)
-            at(SECOND_LAG, tanh_and_store, 1)
             at(FIRST_LAG, first_product, 3)
             at(0, transpose_rows)
             at(FIRST_LAG, keep_clock)
@@ -294,6 +295,8 @@ def tile_quantumneuralnetwork_pa_t_kernel(tc, h0, w1, b1, q1_qw, q1_cw, q1_cb, o
                 out=cw_grouped[:, columns], in_=cw_raw[:, :, columns].rearrange("q t n -> q n t")
             )
 
+        for i in range(5):
+            keep_clock(0)
         transpose_rows(0)
         load_rows(3)
         output_bias = output_bias_column(nc, small, angles, cb)
@@ -303,6 +306,8 @@ def tile_quantumneuralnetwork_pa_t_kernel(tc, h0, w1, b1, q1_qw, q1_cw, q1_cb, o
         quantise_h0(0)
         quantise_w1(0)
         group_w1(1, nc.scalar.copy)
+        for i in range(6):
+            keep_clock(0)
         transpose_rows(1)
         load_rows(4)
         empty_bank(1, 0)

@@ -46,12 +46,11 @@ def quantise(nc, pool, grouped, name):
 def output_bias_column(nc, small, angles, cb):
     diagonal = angles[:].rearrange("q d (i e) -> q (d i) e", e=4)[:, :, 0:4:3]
     turns = small.tile([P, 2, DEPTH * PACK, 2], F32, name="turns")
-    nc.vector.tensor_scalar(
-        out=turns[:, COS], in0=diagonal, scalar1=0.5 / math.pi, scalar2=0.25, op0=ALU.mult, op1=ALU.add
-    )
-    nc.vector.tensor_scalar(
-        out=turns[:, SIN], in0=diagonal, scalar1=0.5 / math.pi, scalar2=0.0, op0=ALU.mult, op1=ALU.add
-    )
+    for kind, quarter in ((COS, 0.25), (SIN, 0.0)):
+        for angle, per_turn in ((THETA, 1.0 / math.pi), (PHI, 0.5 / math.pi)):
+            nc.vector.tensor_scalar(
+                out=turns[:, kind, :, angle], in0=diagonal[:, :, angle], scalar1=per_turn, scalar2=quarter, op0=ALU.mult, op1=ALU.add
+            )
     whole = small.tile([P, 2, DEPTH * PACK, 2], F32, name="whole")
     nc.vector.tensor_scalar(
         out=whole[:], in0=turns[:], scalar1=ROUND_TO_INT, scalar2=ROUND_TO_INT, op0=ALU.add, op1=ALU.subtract
@@ -63,49 +62,35 @@ def output_bias_column(nc, small, angles, cb):
     first_tanh = small.tile([P, 1], F32, name="first_tanh")
     nc.scalar.activation(out=first_tanh[:], in_=part[:, COS, 0, THETA : THETA + 1], func=ACT.Tanh)
 
-    def layer(d):
-        return slice(d * PACK, (d + 1) * PACK)
+    def entry(kind, d, angle):
+        return trig[:, kind, d * PACK : (d + 1) * PACK, angle]
 
-    def rotation(kind, d):
-        return trig[:, kind, layer(d), THETA].unsqueeze(1).to_broadcast([P, 2, PACK])
+    def pair(d, angle):
+        return trig[:, :, d * PACK : (d + 1) * PACK, angle]
 
-    a0 = small.tile([P, 2, PACK], F32, name="a0_first")
-    nc.gpsimd.memset(a0[:, 1, :], 0.0)
-    nc.gpsimd.tensor_copy(out=a0[:, 0, :], in_=trig[:, COS, layer(0), THETA])
-    a1 = small.tile([P, 2, PACK], F32, name="a1_first")
-    nc.gpsimd.tensor_tensor(out=a1[:], in0=trig[:, :, layer(0), PHI], in1=rotation(SIN, 0), op=ALU.mult)
-    for d in range(1, DEPTH):
-        cos_a0 = small.tile([P, 2, PACK], F32)
-        sin_a1 = small.tile([P, 2, PACK], F32)
-        new_a0 = small.tile([P, 2, PACK], F32)
-        nc.gpsimd.tensor_tensor(out=cos_a0[:], in0=a0[:], in1=rotation(COS, d), op=ALU.mult)
-        nc.gpsimd.tensor_tensor(out=sin_a1[:], in0=a1[:], in1=rotation(SIN, d), op=ALU.mult)
-        nc.gpsimd.tensor_tensor(out=new_a0[:], in0=cos_a0[:], in1=sin_a1[:], op=ALU.subtract)
-        if d < DEPTH - 1:
-            sin_a0 = small.tile([P, 2, PACK], F32)
-            cos_a1 = small.tile([P, 2, PACK], F32)
-            turned = small.tile([P, 2, PACK], F32)
-            nc.gpsimd.tensor_tensor(out=sin_a0[:], in0=a0[:], in1=rotation(SIN, d), op=ALU.mult)
-            nc.gpsimd.tensor_tensor(out=cos_a1[:], in0=a1[:], in1=rotation(COS, d), op=ALU.mult)
-            nc.gpsimd.tensor_tensor(out=turned[:], in0=sin_a0[:], in1=cos_a1[:], op=ALU.add)
-            by_cos = small.tile([P, 2, PACK], F32)
-            by_sin = small.tile([P, 2, PACK], F32)
-            new_a1 = small.tile([P, 2, PACK], F32)
-            cos_phi = trig[:, COS, layer(d), PHI].unsqueeze(1).to_broadcast([P, 2, PACK])
-            sin_phi = trig[:, SIN, layer(d), PHI].unsqueeze(1).to_broadcast([P, 2, PACK])
-            nc.gpsimd.tensor_tensor(out=by_cos[:], in0=turned[:], in1=cos_phi, op=ALU.mult)
-            nc.gpsimd.tensor_tensor(out=by_sin[:], in0=turned[:], in1=sin_phi, op=ALU.mult)
-            nc.gpsimd.tensor_tensor(out=new_a1[:, 0, :], in0=by_cos[:, 0, :], in1=by_sin[:, 1, :], op=ALU.subtract)
-            nc.gpsimd.tensor_tensor(out=new_a1[:, 1, :], in0=by_sin[:, 0, :], in1=by_cos[:, 1, :], op=ALU.add)
-            a1 = new_a1
-        a0 = new_a0
-    squares = small.tile([P, 2, PACK], F32, name="squares")
-    nc.gpsimd.tensor_tensor(out=squares[:], in0=a0[:], in1=a0[:], op=ALU.mult)
+    def both(column):
+        return column.unsqueeze(1).to_broadcast([P, 2, PACK])
+
+    def combine(a, b, op, name, shape=(P, PACK)):
+        result = small.tile(list(shape), F32, name=name)
+        nc.gpsimd.tensor_tensor(out=result[:], in0=a, in1=b, op=op)
+        return result
+
+    xy = combine(pair(0, PHI), both(entry(SIN, 0, THETA)), ALU.mult, "xy", (P, 2, PACK))
+    sin_x = combine(entry(SIN, 1, THETA), xy[:, 0], ALU.mult, "sin_x")
+    cos_x = combine(entry(COS, 1, THETA), xy[:, 0], ALU.mult, "cos_x")
+    zx = combine(pair(1, THETA), both(entry(COS, 0, THETA)), ALU.mult, "zx", (P, 2, PACK))
+    x1 = combine(zx[:, 1], cos_x[:], ALU.add, "x1")
+    y_sin = combine(xy[:, 1], entry(SIN, 1, PHI), ALU.mult, "y_sin")
+    x_cos = combine(x1[:], entry(COS, 1, PHI), ALU.mult, "x_cos")
+    z1 = combine(zx[:, 0], sin_x[:], ALU.subtract, "z1")
+    x2 = combine(x_cos[:], y_sin[:], ALU.subtract, "x2")
+    z_cos = combine(z1[:], entry(COS, 2, THETA), ALU.mult, "z_cos")
+    x_sin = combine(x2[:], entry(SIN, 2, THETA), ALU.mult, "x_sin")
+    z2 = combine(z_cos[:], x_sin[:], ALU.subtract, "z2")
     prob = small.tile([P, PACK], F32, name="prob")
-    nc.gpsimd.tensor_tensor(out=prob[:], in0=squares[:, 0, :], in1=squares[:, 1, :], op=ALU.add)
-    bias_column = small.tile([P, PACK], F32, name="bias_column")
-    nc.gpsimd.tensor_tensor(out=bias_column[:], in0=prob[:], in1=cb[:], op=ALU.add)
-    return bias_column
+    nc.gpsimd.tensor_scalar(out=prob[:], in0=z2[:], scalar1=0.5, scalar2=0.5, op0=ALU.mult, op1=ALU.add)
+    return combine(prob[:], cb[:], ALU.add, "bias_column")
 
 
 def tile_quantumneuralnetwork_pa_t_kernel(tc, h0, w1, b1, q1_qw, q1_cw, q1_cb, out):

@@ -135,7 +135,7 @@ def tile_quantumneuralnetwork_pa_t_kernel(tc, h0, w1, b1, q1_qw, q1_cw, q1_cb, o
         load_rows(2)
 
         blank = keep.tile([P, ROWS], BF16, name="blank")
-        nc.vector.memset(blank[:], 0.0)
+        nc.gpsimd.memset(blank[:].bitcast(F32), 0.0)
         ident = keep.tile([P, P], F32, name="ident")
         make_identity(nc, ident[:])
         first_sin = small.tile([P, 1], F32, name="first_sin")
@@ -280,7 +280,7 @@ def tile_quantumneuralnetwork_pa_t_kernel(tc, h0, w1, b1, q1_qw, q1_cw, q1_cb, o
                 out=cw_grouped[:, columns], in_=cw_raw[:, :, columns].rearrange("q t n -> q n t")
             )
 
-        for i in range(5):
+        for i in range(4):
             keep_clock(0)
         transpose_rows(0)
         load_rows(3)

@@ -257,8 +257,11 @@ def tile_quantumneuralnetwork_pa_t_kernel(tc, h0, w1, b1, q1_qw, q1_cw, q1_cb, o
             at(SECOND_LAG, quantise_h1)
             at(REGROUP_LAG, regroup_h1)
             at(COPY_LAG, empty_bank, 0)
-            at(COPY_LAG, empty_bank, 1)
+            if not (step in (6, 11)):
+                at(COPY_LAG, empty_bank, 1)
             at(TANH_LAG, tanh_and_store, 2, 2)
+            if step in (6, 11):
+                at(COPY_LAG, empty_bank, 1, nc.scalar.copy)
             at(FIRST_LAG, first_product, 0)
             at(SECOND_LAG, second_product, 0)
             at(FIRST_LAG, first_product, 1)
@@ -282,6 +285,19 @@ def tile_quantumneuralnetwork_pa_t_kernel(tc, h0, w1, b1, q1_qw, q1_cw, q1_cb, o
 
         for i in range(4):
             keep_clock(0)
+        def group_cw_aside(half):
+            columns = slice(half * H // 2, (half + 1) * H // 2)
+            go = small.tile([P, 1], F32, name="go")
+            nc.vector.memset(go[:], 1.0)
+            nc.gpsimd.tensor_scalar(
+                out=cw_grouped[:, columns],
+                in0=cw_raw[:, :, columns].rearrange("q t n -> q n t"),
+                scalar1=go[:],
+                scalar2=0.0,
+                op0=ALU.mult,
+                op1=ALU.add,
+            )
+
         transpose_rows(0)
         load_rows(3)
         output_bias = output_bias_column(nc, small, angles, cb)
@@ -306,10 +322,10 @@ def tile_quantumneuralnetwork_pa_t_kernel(tc, h0, w1, b1, q1_qw, q1_cw, q1_cb, o
         group_cw(0)
         for t in range(PACK):
             first_product(1, t)
+        group_cw_aside(1)
         empty_bank(2, 0)
         empty_bank(2, 1)
         quantise_h0(2)
-        group_cw(1)
         spread = psum_2.tile([P, PACK, P], F32, name="spread", tag="product2")
         for i in range(PACK):
             nc.tensor.matmul(

@@ -205,8 +205,8 @@ def tile_quantumneuralnetwork_pa_t_kernel(tc, h0, w1, b1, q1_qw, q1_cw, q1_cb, o
                 out=h1_planes[g][:, t, :], in_=product1[:], func=ACT.Relu, bias=b1_column[:, t : t + 1], scale=1.0
             )
 
-        def keep_clock(g):
-            unread = psum_1.tile([P, ROWS], F32, name="unread", tag="product1")
+        def keep_clock(g, pool=psum_1, tag="product1"):
+            unread = pool.tile([P, ROWS], F32, name="unread", tag=tag)
             nc.tensor.matmul(out=unread[:], lhsT=blank[:, :P], rhs=blank[:], start=True, stop=True)
 
         def regroup_h1(g, engine=nc.gpsimd, pool=single):
@@ -221,7 +221,16 @@ def tile_quantumneuralnetwork_pa_t_kernel(tc, h0, w1, b1, q1_qw, q1_cw, q1_cb, o
             )
 
         def quantise_h1(g):
-            h1_packed[g] = quantise(nc, work, h1_grouped[g][:].rearrange("q c t -> q (c t)"), "h1")
+            words = work.tile([P, ROWS], U32, name="h1_words", align_bytes=64)
+            scales = work.tile([P, ROWS], U8, name="h1_scales", align_bytes=64)
+            for start in range(0, ROWS, ROWS // 2):
+                part = slice(start, start + ROWS // 2)
+                nc.vector.quantize_mx(
+                    out=words[:, part].bitcast(FP8X4),
+                    scales=scales[:, part],
+                    in_=h1_grouped[g][:, part].rearrange("q c t -> q (c t)"),
+                )
+            h1_packed[g] = (words, scales)
 
         def second_product(g, r):
             h1_words, h1_scales = h1_packed[g]
@@ -356,6 +365,8 @@ def tile_quantumneuralnetwork_pa_t_kernel(tc, h0, w1, b1, q1_qw, q1_cw, q1_cb, o
         tanh_and_store(last - 3, 2)
         quantise_h1(last - 2)
         regroup_h1(last - 1)
+        for i in range(3):
+            keep_clock(last, psum_t, "flipped")
         for i in range(PACK):
             first_product(last, i)
             second_product(last - 2, i)

import math
from contextlib import ExitStack

import concourse.mybir as mybir
from concourse.masks import make_identity

F32 = mybir.dt.float32
BF16 = mybir.dt.bfloat16
U32 = mybir.dt.uint32
U8 = mybir.dt.uint8
FP8X4 = mybir.dt.float8_e4m3fn_x4
ACT = mybir.ActivationFunctionType
ALU = mybir.AluOpType

P = 128
PACK = 4
BATCH = 8192
H = P * PACK
DEPTH = 3
ROWS = 512
SUB = ROWS // P
ROUNDS = BATCH // ROWS
ROUND_TO_INT = 1.5 * 2.0**23
COS = 0
SIN = 1
THETA = 0
PHI = 1
COPY_LAG = 1
FIRST_LAG = 2
REGROUP_LAG = 3
TANH_LAG = 5
ROWS_AHEAD = 2
SECOND_LAG = 4

FLOPS = 2 * 2 * BATCH * H * H


def quantise(nc, pool, grouped, name):
    columns = grouped.shape[1] // PACK
    words = pool.tile([P, columns], U32, name=name + "_words", align_bytes=64)
    scales = pool.tile([P, columns], U8, name=name + "_scales", align_bytes=64)
    nc.vector.quantize_mx(out=words[:].bitcast(FP8X4), scales=scales[:], in_=grouped)
    return words, scales


def output_bias_column(nc, small, angles, cb):
    diagonal = angles[:].rearrange("q d (i e) -> q (d i) e", e=4)[:, :, 0:4:3]
    turns = small.tile([P, 2, DEPTH * PACK, 2], F32, name="turns")
    for kind, quarter in ((COS, 0.25), (SIN, 0.0)):
        for angle, per_turn in ((THETA, 1.0 / math.pi), (PHI, 0.5 / math.pi)):
            nc.vector.tensor_scalar(
                out=turns[:, kind, :, angle], in0=diagonal[:, :, angle], scalar1=per_turn, scalar2=quarter, op0=ALU.mult, op1=ALU.add
            )
    whole = small.tile([P, 2, DEPTH * PACK, 2], F32, name="whole")
    nc.vector.tensor_scalar(
        out=whole[:], in0=turns[:], scalar1=ROUND_TO_INT, scalar2=ROUND_TO_INT, op0=ALU.add, op1=ALU.subtract
    )
    part = small.tile([P, 2, DEPTH * PACK, 2], F32, name="part")
    nc.vector.tensor_tensor(out=part[:], in0=turns[:], in1=whole[:], op=ALU.subtract)
    trig = small.tile([P, 2, DEPTH * PACK, 2], F32, name="trig")
    nc.scalar.activation(out=trig[:], in_=part[:], func=ACT.Sin, scale=2.0 * math.pi)
    first_tanh = small.tile([P, 1], F32, name="first_tanh")
    nc.scalar.activation(out=first_tanh[:], in_=part[:, COS, 0, THETA : THETA + 1], func=ACT.Tanh)

    def entry(kind, d, angle):
        return trig[:, kind, d * PACK : (d + 1) * PACK, angle]

    def pair(d, angle):
        return trig[:, :, d * PACK : (d + 1) * PACK, angle]

    def both(column):
        return column.unsqueeze(1).to_broadcast([P, 2, PACK])

    def combine(a, b, op, name, shape=(P, PACK)):
        result = small.tile(list(shape), F32, name=name)
        nc.gpsimd.tensor_tensor(out=result[:], in0=a, in1=b, op=op)
        return result

    xy = combine(pair(0, PHI), both(entry(SIN, 0, THETA)), ALU.mult, "xy", (P, 2, PACK))
    sin_x = combine(entry(SIN, 1, THETA), xy[:, 0], ALU.mult, "sin_x")
    cos_x = combine(entry(COS, 1, THETA), xy[:, 0], ALU.mult, "cos_x")
    zx = combine(pair(1, THETA), both(entry(COS, 0, THETA)), ALU.mult, "zx", (P, 2, PACK))
    x1 = combine(zx[:, 1], cos_x[:], ALU.add, "x1")
    y_sin = combine(xy[:, 1], entry(SIN, 1, PHI), ALU.mult, "y_sin")
    x_cos = combine(x1[:], entry(COS, 1, PHI), ALU.mult, "x_cos")
    z1 = combine(zx[:, 0], sin_x[:], ALU.subtract, "z1")
    x2 = combine(x_cos[:], y_sin[:], ALU.subtract, "x2")
    z_cos = combine(z1[:], entry(COS, 2, THETA), ALU.mult, "z_cos")
    x_sin = combine(x2[:], entry(SIN, 2, THETA), ALU.mult, "x_sin")
    z2 = combine(z_cos[:], x_sin[:], ALU.subtract, "z2")
    prob = small.tile([P, PACK], F32, name="prob")
    nc.gpsimd.tensor_scalar(out=prob[:], in0=z2[:], scalar1=0.5, scalar2=0.5, op0=ALU.mult, op1=ALU.add)
    return combine(prob[:], cb[:], ALU.add, "bias_column")


def tile_quantumneuralnetwork_pa_t_kernel(tc, h0, w1, b1, q1_qw, q1_cw, q1_cb, out):
    nc = tc.nc
    with ExitStack() as ctx:
        ctx.enter_context(tc.manual_schedule())
        keep = ctx.enter_context(tc.tile_pool(name="keep", bufs=1))
        small = ctx.enter_context(tc.tile_pool(name="small", bufs=2))
        rows_in = ctx.enter_context(tc.tile_pool(name="rows_in", bufs=ROWS_AHEAD + 1))
        work = ctx.enter_context(tc.tile_pool(name="work", bufs=3))
        single = ctx.enter_context(tc.tile_pool(name="single", bufs=1))
        rows_out = ctx.enter_context(tc.tile_pool(name="rows_out", bufs=4))
        psum_t = ctx.enter_context(tc.psum_pool(name="psum_t", bufs=2))
        psum_1 = ctx.enter_context(tc.psum_pool(name="psum_1", bufs=3))
        psum_2 = ctx.enter_context(tc.psum_pool(name="psum_2", bufs=3))

        h0_rounds = h0.rearrange("(g c r) k -> g c (r k)", c=P, r=SUB)
        out_rounds = out.rearrange("(g c r) n -> g c r n", c=P, r=SUB)

        angles = small.tile([P, DEPTH, PACK * 4], BF16, name="angles")
        nc.sync.dma_start(out=angles[:], in_=q1_qw.rearrange("d (q i) a b -> q d (i a b)", i=PACK))
        x_tiles = {}

        def load_rows(g, pieces=1):
            x_tiles[g] = rows_in.tile([P, SUB * H], BF16, name="x")
            width = SUB * H // pieces
            for start in range(0, SUB * H, width):
                nc.sync.dma_start(
                    out=x_tiles[g][:, start : start + width], in_=h0_rounds[g][:, start : start + width]
                )

        load_rows(0, 2)
        w1_raw = keep.tile([P, PACK, H], BF16, name="w1_raw")
        nc.sync.dma_start(out=w1_raw[:], in_=w1.rearrange("(q t) j -> q t j", t=PACK))
        b1_column = keep.tile([P, PACK], BF16, name="b1_column")
        nc.sync.dma_start(out=b1_column[:], in_=b1.rearrange("(q t) -> q t", t=PACK))
        cb = small.tile([P, PACK], BF16, name="cb")
        nc.sync.dma_start(out=cb[:], in_=q1_cb.rearrange("(q i) -> q i", i=PACK))
        load_rows(1)
        cw_raw = keep.tile([P, PACK, H], BF16, name="cw_raw")
        nc.sync.dma_start(out=cw_raw[:], in_=q1_cw.rearrange("(q t) n -> q t n", t=PACK))
        load_rows(2)

        blank = keep.tile([P, ROWS], BF16, name="blank")
        nc.gpsimd.memset(blank[:].bitcast(F32), 0.0)
        ident = keep.tile([P, P], F32, name="ident")
        make_identity(nc, ident[:])
        first_sin = small.tile([P, 1], F32, name="first_sin")
        nc.scalar.activation(out=first_sin[:], in_=blank[:, :1], func=ACT.Sin)

        w1_grouped = keep.tile([P, H, PACK], BF16, name="w1_grouped", align_bytes=64)
        w1_words = keep.tile([P, H], U32, name="w1_words", align_bytes=64)
        w1_scales = keep.tile([P, H], U8, name="w1_scales", align_bytes=64)

        def group_w1(half, copy=nc.vector.tensor_copy):
            columns = slice(half * H // 2, (half + 1) * H // 2)
            copy(
                out=w1_grouped[:, columns].rearrange("q (t m) k -> q t m k", m=P),
                in_=w1_raw[:].rearrange("q k (m t) -> q t m k", t=PACK)[:, 2 * half : 2 * half + 2],
            )

        def quantise_w1(half):
            columns = slice(half * H // 2, (half + 1) * H // 2)
            nc.vector.quantize_mx(
                out=w1_words[:, columns].bitcast(FP8X4),
                scales=w1_scales[:, columns],
                in_=w1_grouped[:, columns].rearrange("q j k -> q (j k)"),
            )

        flipped, h0_grouped, h0_packed, h1_planes, h1_grouped, h1_packed, results = {}, {}, {}, {}, {}, {}, {}

        def transpose_rows(g, halves=(0, 1)):
            x_words = x_tiles[g][:].bitcast(F32)
            for half in halves:
                flipped[g, half] = psum_t.tile([P, 2, 2, P], F32, name="flipped")
                for r in range(2):
                    for u in range(2):
                        row = (2 * half + r) * 2 * P
                        nc.tensor.transpose(
                            out=flipped[g, half][:, r, u, :],
                            in_=x_words[:, row + u : row + 2 * P : 2],
                            identity=ident[:],
                        )

        def empty_bank(g, half, copy=nc.vector.tensor_copy):
            if half == 0:
                h0_grouped[g] = work.tile([P, ROWS * PACK], BF16, name="h0_grouped", align_bytes=64)
            h0_pairs = h0_grouped[g][:].bitcast(F32).rearrange("q (h r c u) -> q h r c u", h=2, r=2, u=2)
            copy(out=h0_pairs[:, half], in_=flipped[g, half][:].rearrange("q r u c -> q r c u"))

        def quantise_h0(g):
            h0_packed[g] = quantise(nc, work, h0_grouped[g][:], "h0")

        def first_product(g, t):
            h0_words, h0_scales = h0_packed[g]
            if t == 0:
                h1_planes[g] = work.tile([P, PACK, ROWS], BF16, name="h1_planes")
            if g < 2 and t == PACK - 1:
                product1 = psum_2.tile([P, ROWS], F32, name="product1", tag="product2")
            else:
                product1 = psum_1.tile([P, ROWS], F32, name="product1")
            nc.tensor.matmul_mx(
                out=product1[:],
                lhsT=w1_words[:, t * P : (t + 1) * P].bitcast(FP8X4),
                lhsT_scale=w1_scales[:, t * P : (t + 1) * P],
                rhs=h0_words[:].bitcast(FP8X4),
                rhs_scale=h0_scales[:],
                start=True,
                stop=True,
            )
            nc.scalar.activation(
                out=h1_planes[g][:, t, :], in_=product1[:], func=ACT.Relu, bias=b1_column[:, t : t + 1], scale=1.0
            )

        def keep_clock(g, pool=psum_1, tag="product1"):
            unread = pool.tile([P, ROWS], F32, name="unread", tag=tag)
            nc.tensor.matmul(out=unread[:], lhsT=blank[:, :P], rhs=blank[:], start=True, stop=True)

        def regroup_h1(g, engine=nc.gpsimd, pool=single):
            h1_grouped[g] = pool.tile([P, ROWS, PACK], BF16, name="h1_grouped", align_bytes=64)
            engine.tensor_scalar(
                out=h1_grouped[g][:].rearrange("q (c i) t -> q c t i", i=4),
                in0=h1_planes[g][:].rearrange("q t (c i) -> q c t i", i=4),
                scalar1=1.0,
                scalar2=0.0,
                op0=ALU.mult,
                op1=ALU.add,
            )

        def quantise_h1(g):
            words = work.tile([P, ROWS], U32, name="h1_words", align_bytes=64)
            scales = work.tile([P, ROWS], U8, name="h1_scales", align_bytes=64)
            for start in range(0, ROWS, ROWS // 2):
                part = slice(start, start + ROWS // 2)
                nc.vector.quantize_mx(
                    out=words[:, part].bitcast(FP8X4),
                    scales=scales[:, part],
                    in_=h1_grouped[g][:, part].rearrange("q c t -> q (c t)"),
                )
            h1_packed[g] = (words, scales)

        def second_product(g, r):
            h1_words, h1_scales = h1_packed[g]
            if r == 0:
                results[g] = rows_out.tile([P, SUB, H], F32, name="y")
            product2 = psum_2.tile([P, H], F32, name="product2")
            nc.tensor.matmul_mx(
                out=product2[:],
                lhsT=h1_words[:, r * P : (r + 1) * P].bitcast(FP8X4),
                lhsT_scale=h1_scales[:, r * P : (r + 1) * P],
                rhs=cw_words[:].bitcast(FP8X4),
                rhs_scale=cw_scales[:],
                start=True,
                stop=True,
            )
            nc.vector.tensor_tensor(out=results[g][:, r, :], in0=product2[:], in1=bias_row[:], op=ALU.add)

        def tanh_and_store(g, r, count=1):
            part = results[g][:, r : r + count, :]
            nc.scalar.activation(out=part, in_=part, func=ACT.Tanh)
            nc.sync.dma_start(out=out_rounds[g][:, r : r + count, :], in_=part)

        AHEAD = {transpose_rows: 4, empty_bank: 4, quantise_h0: 3, first_product: 3, regroup_h1: 2, quantise_h1: 1}

        AHEAD[load_rows] = 6

        def pipeline_step(step):
            def at(lag, stage, *args):
                if AHEAD.get(stage, 0) <= step - lag < ROUNDS:
                    stage(step - lag, *args)

            at(-ROWS_AHEAD, load_rows)
            at(SECOND_LAG, quantise_h1)
            at(REGROUP_LAG, regroup_h1)
            at(COPY_LAG, empty_bank, 0)
            if not (step in (6, 11)):
                at(COPY_LAG, empty_bank, 1)
            at(TANH_LAG, tanh_and_store, 2, 2)
            if step in (6, 11):
                at(COPY_LAG, empty_bank, 1, nc.scalar.copy)
            at(FIRST_LAG, first_product, 0)
            at(SECOND_LAG, second_product, 0)
            at(FIRST_LAG, first_product, 1)
            at(SECOND_LAG, second_product, 1)
            at(FIRST_LAG, first_product, 2)
            at(SECOND_LAG, second_product, 2)
            at(SECOND_LAG, tanh_and_store, 0, 2)
            at(SECOND_LAG, second_product, 3)
            at(FIRST_LAG, first_product, 3)
            at(0, transpose_rows)
            at(FIRST_LAG, keep_clock)
            at(COPY_LAG, quantise_h0)

        cw_grouped = keep.tile([P, H, PACK], BF16, name="cw_grouped", align_bytes=64)

        def group_cw(half):
            columns = slice(half * H // 2, (half + 1) * H // 2)
            nc.vector.tensor_copy(
                out=cw_grouped[:, columns], in_=cw_raw[:, :, columns].rearrange("q t n -> q n t")
            )

        for i in range(4):
            keep_clock(0)
        def group_cw_aside(half):
            columns = slice(half * H // 2, (half + 1) * H // 2)
            go = small.tile([P, 1], F32, name="go")
            nc.vector.memset(go[:], 1.0)
            nc.gpsimd.tensor_scalar(
                out=cw_grouped[:, columns],
                in0=cw_raw[:, :, columns].rearrange("q t n -> q n t"),
                scalar1=go[:],
                scalar2=0.0,
                op0=ALU.mult,
                op1=ALU.add,
            )

        transpose_rows(0)
        load_rows(3)
        output_bias = output_bias_column(nc, small, angles, cb)
        empty_bank(0, 0)
        empty_bank(0, 1, nc.scalar.copy)
        group_w1(0)
        quantise_h0(0)
        quantise_w1(0)
        group_w1(1, nc.scalar.copy)
        for i in range(6):
            keep_clock(0)
        transpose_rows(1)
        load_rows(4)
        empty_bank(1, 0)
        quantise_w1(1)
        for t in range(PACK):
            first_product(0, t)
        empty_bank(1, 1)
        transpose_rows(2)
        load_rows(5)
        quantise_h0(1)
        group_cw(0)
        for t in range(PACK):
            first_product(1, t)
        group_cw_aside(1)
        empty_bank(2, 0)
        empty_bank(2, 1)
        quantise_h0(2)
        spread = psum_2.tile([P, PACK, P], F32, name="spread", tag="product2")
        for i in range(PACK):
            nc.tensor.matmul(
                out=spread[:, i, :],
                lhsT=output_bias[:, i : i + 1].to_broadcast([P, P]),
                rhs=ident[:],
                start=True,
                stop=True,
            )
        for t in range(PACK - 1):
            first_product(2, t)
        transpose_rows(3)
        first_product(2, PACK - 1)
        regroup_h1(0, nc.vector)
        cw_words, cw_scales = quantise(nc, keep, cw_grouped[:].rearrange("q n t -> q (n t)"), "cw")
        quantise_h1(0)
        bias_row = keep.tile([P, H], F32, name="bias_row")
        nc.vector.tensor_copy(
            out=bias_row[:].rearrange("p (q i) -> p q i", i=PACK), in_=spread[:].rearrange("p i q -> p q i")
        )
        regroup_h1(1)
        empty_bank(3, 0, nc.scalar.copy)
        empty_bank(3, 1, nc.scalar.copy)
        for step in range(SECOND_LAG, ROUNDS + COPY_LAG):
            pipeline_step(step)

        last = ROUNDS - 1
        tanh_and_store(last - 3, 2)
        quantise_h1(last - 2)
        regroup_h1(last - 1)
        for i in range(3):
            keep_clock(last, psum_t, "flipped")
        for i in range(PACK):
            first_product(last, i)
            second_product(last - 2, i)
        tanh_and_store(last - 3, 3)
        for r in range(SUB):
            tanh_and_store(last - 2, r)
        quantise_h1(last - 1)
        regroup_h1(last, nc.vector, work)
        for r in range(SUB):
            second_product(last - 1, r)
            tanh_and_store(last - 1, r)
            if r == 0:
                quantise_h1(last)
        for r in range(SUB):
            second_product(last, r)
            tanh_and_store(last, r)
